import numpy as np
import ml_dtypes


def mxq(x, axis, fmt="e4m3"):
    dtype, down = {"e4m3": (ml_dtypes.float8_e4m3fn, 7), "e5m2": (ml_dtypes.float8_e5m2, 14)}[fmt]
    v = np.moveaxis(np.asarray(x, np.float32).astype(ml_dtypes.bfloat16).astype(np.float64), axis, -1)
    blocks = v.reshape(v.shape[:-1] + (-1, 32))
    amax = np.abs(blocks).max(-1, keepdims=True)
    byte = np.maximum(np.where(amax > 0, np.frexp(amax)[1] - 1 + 127, 0) - down, 1)
    scale = np.exp2(byte - 127.0)
    codes = (blocks / scale).astype(np.float32).astype(dtype).astype(np.float64)
    return np.moveaxis((codes * scale).reshape(v.shape), -1, axis)


WIDE = False


def mx_kscale(k):
    if not WIDE:
        return np.ones(k)
    levels = np.array([10, -10, 5, -5, 0])
    a = np.random.permutation(np.resize(levels, k // 512 * 4)).reshape(k // 512, 4)
    idx = np.arange(k)
    return np.exp2(a[idx // 512, idx % 128 // 32])


BF16 = ml_dtypes.bfloat16


def bf(x):
    return np.asarray(x, np.float32).astype(BF16)


def f64(x):
    return np.asarray(x).astype(np.float64)


E2M1 = np.array([0.0, 0.5, 1.0, 1.5, 2.0, 3.0, 4.0, 6.0, -0.0, -0.5, -1.0, -1.5, -2.0, -3.0, -4.0, -6.0])


def pack_weight(w, fmt):
    k, n = w.shape
    w = f64(bf(w)).reshape(k // 32, 32, n)
    amax = np.abs(w).max(1)
    if fmt == "e4m3":
        byte = np.frexp(amax)[1] - 1 + 127 - 7
    else:
        mant, ex = np.frexp(amax / 6.0)
        byte = np.where(mant > 0.5, ex, ex - 1) + 127
    byte = np.clip(np.where(amax > 0, byte, 1), 1, 254)
    scaled = (w * np.exp2(127.0 - byte)[:, None, :]).reshape(k, n).astype(np.float32)
    by_word = np.ascontiguousarray(scaled.reshape(k // 512, 128, 4, n).transpose(0, 1, 3, 2))
    if fmt == "e4m3":
        words = by_word.astype(ml_dtypes.float8_e4m3fn).view(np.uint8)
    else:
        c = by_word.astype(ml_dtypes.float4_e2m1fn).view(np.uint8) & 0xF
        words = c[..., 0::2] | (c[..., 1::2] << 4)
    return np.ascontiguousarray(words), np.ascontiguousarray(byte.astype(np.uint8).reshape(k // 512, 16, n))


def unpack_weight(words, scales, fmt):
    g, p, n, _ = words.shape
    if fmt == "e4m3":
        vals = np.ascontiguousarray(words).view(ml_dtypes.float8_e4m3fn).astype(np.float64)
    else:
        nib = np.empty((g, p, n, 4), np.uint8)
        nib[..., 0::2] = words & 0xF
        nib[..., 1::2] = words >> 4
        vals = E2M1[nib]
    vals = vals * np.repeat(np.exp2(scales.astype(np.float64) - 127.0), 8, axis=1)[..., None]
    return vals.transpose(0, 1, 3, 2).reshape(g * 512, n)

def pack4(w):
    words, scales = pack_weight(w, "e2m1")
    return words.reshape(words.shape[0], 128, -1), scales


def unpack4(words, scales):
    return unpack_weight(words.reshape(words.shape[0], 128, -1, 2), scales, "e2m1")


B, S, I, Q = 512, 8, 1024, 1024
LN_EPS = 1e-5


def setup_inputs():
    s = mx_kscale(I)
    language_features = bf(np.random.standard_normal((B, I)) * s)
    stack = np.random.standard_normal((S, I, Q)) / np.sqrt(I) / s[None, :, None]
    W_words, W_scales = pack4(stack.reshape(-1, Q))
    return {"language_features": language_features,
            "W_words": W_words,
            "W_scales": W_scales,
            "b": bf(np.random.standard_normal((S, Q)) * 0.2),
            "amplitude_weights": bf(np.random.standard_normal((S, Q))),
            "phase_weights": bf(np.random.standard_normal((S, Q))),
            "ln_gamma": bf(1.0 + 0.1 * np.random.standard_normal(Q)),
            "ln_beta": bf(0.1 * np.random.standard_normal(Q))}


def reference(language_features, W_words, W_scales, b, amplitude_weights, phase_weights, ln_gamma, ln_beta):
    xq = mxq(f64(language_features), 1, "e4m3")
    wq = unpack4(W_words, W_scales).reshape(S, I, Q)
    states = (xq @ wq).transpose(1, 0, 2) + f64(b)[None, :, :]
    a = f64(amplitude_weights)
    e = np.exp(a - a.max(axis=0, keepdims=True))
    amplitudes = e / e.sum(axis=0, keepdims=True)
    mix = amplitudes * np.cos(f64(phase_weights))
    sup = states * mix[None, :, :]
    mean = sup.mean(axis=-1, keepdims=True)
    var = sup.var(axis=-1, keepdims=True)
    return (sup - mean) * (1.0 / np.sqrt(var + LN_EPS)) * f64(ln_gamma) + f64(ln_beta)

@@ -1,0 +1,258 @@
+import math
+from contextlib import ExitStack
+
+import concourse.mybir as mybir
+from concourse.masks import make_identity
+
+F32 = mybir.dt.float32
+BF16 = mybir.dt.bfloat16
+I32 = mybir.dt.int32
+U32 = mybir.dt.uint32
+U8 = mybir.dt.uint8
+FP8X4 = mybir.dt.float8_e4m3fn_x4
+FP4X4 = mybir.dt.float4_e2m1fn_x4
+ALU = mybir.AluOpType
+ACT = mybir.ActivationFunctionType
+AXIS = mybir.AxisListType
+
+P = 128
+ROWS = 512
+STATES = 8
+K = 1024
+Q = 1024
+K_PASS = 4 * P
+PASSES = K // K_PASS
+ROW_TILES = ROWS // P
+Q_TILES = Q // P
+BANK = 512
+HALVES = Q // BANK
+TILES_PER_BANK = BANK // P
+MIX_COLS = STATES * Q_TILES
+Q_TILES_PER_STEP = Q_TILES // ROW_TILES
+BN_STATS_DIM = 6
+LN_EPS = 1e-5
+
+FLOPS = 2 * ROWS * STATES * K * Q
+
+
+def tile_quantumsuperposition_e_kernel(
+    tc,
+    language_features,
+    W_words,
+    W_scales,
+    b,
+    amplitude_weights,
+    phase_weights,
+    ln_gamma,
+    ln_beta,
+    out,
+):
+    nc = tc.nc
+    with ExitStack() as ctx:
+        keep = ctx.enter_context(tc.tile_pool(name="keep", bufs=1))
+
+        ident_f32 = keep.tile([P, P], F32)
+        make_identity(nc, ident_f32[:])
+        ident_bf16 = keep.tile([P, P], BF16)
+        make_identity(nc, ident_bf16[:])
+        eps = keep.tile([P, 1], F32)
+        nc.vector.memset(eps[:], LN_EPS)
+
+        w_words = keep.tile([P, STATES * PASSES, 2 * Q], U8, align_bytes=64)
+        w_scales = keep.tile([P, STATES * PASSES, Q], U8, align_bytes=64)
+        x_codes = keep.tile([P, PASSES, ROWS], U32, align_bytes=64)
+        x_scales = keep.tile([P, PASSES, ROWS], U8, align_bytes=64)
+
+        mix = keep.tile([P, MIX_COLS], F32)
+        mixed_bias = keep.tile([P, MIX_COLS], F32)
+        gamma_all = keep.tile([P, Q], BF16)
+        beta_all = keep.tile([P, Q], BF16)
+
+        with tc.tile_pool(name="head", bufs=1) as head, tc.psum_pool(name="head_psum", bufs=1) as head_psum:
+            x_rows = head.tile([P, ROW_TILES, K], BF16)
+            for m in range(ROW_TILES):
+                nc.sync.dma_start(out=x_rows[:, m, :], in_=language_features[P * m : P * (m + 1), :])
+
+            for s in range(STATES):
+                groups = slice(PASSES * s, PASSES * (s + 1))
+                nc.sync.dma_start(
+                    out=w_words[:, groups, :].bitcast(I32),
+                    in_=W_words[groups].rearrange("g p c -> p g c").bitcast(I32),
+                )
+                nc.vector.memset(w_scales[:, groups, :].bitcast(I32), 0)
+                for i in range(4):
+                    nc.sync.dma_start(
+                        out=w_scales[32 * i : 32 * i + 4, groups, :].bitcast(I32),
+                        in_=W_scales[groups, 4 * i : 4 * i + 4, :].rearrange("g r n -> r g n").bitcast(I32),
+                    )
+
+            amp_phase_rows = head.tile([P, P], BF16)
+            bias_rows = head.tile([P, P], BF16)
+            nc.vector.memset(bias_rows[MIX_COLS:P, :], 0.0)
+            nc.scalar.dma_start(
+                out=amp_phase_rows[0:MIX_COLS, :], in_=amplitude_weights.rearrange("s (t q) -> (s t) q", q=P)
+            )
+            nc.scalar.dma_start(
+                out=amp_phase_rows[MIX_COLS:P, :], in_=phase_weights.rearrange("s (t q) -> (s t) q", q=P)
+            )
+            nc.scalar.dma_start(out=bias_rows[0:MIX_COLS, :], in_=b.rearrange("s (t q) -> (s t) q", q=P))
+            nc.scalar.dma_start(out=gamma_all[:], in_=ln_gamma.partition_broadcast(P))
+            nc.scalar.dma_start(out=beta_all[:], in_=ln_beta.partition_broadcast(P))
+
+            table_cols = head_psum.tile([P, 4, MIX_COLS], BF16)
+            nc.tensor.transpose(
+                out=table_cols[:, 0:2, :].rearrange("p a c -> p (a c)"), in_=amp_phase_rows[:], identity=ident_bf16[:]
+            )
+            nc.tensor.transpose(
+                out=table_cols[:, 2:4, :].rearrange("p a c -> p (a c)"), in_=bias_rows[:], identity=ident_bf16[:]
+            )
+            tables = head.tile([P, 3, MIX_COLS], F32)
+            nc.vector.tensor_copy(out=tables[:], in_=table_cols[:, 0:3, :])
+            amplitude = tables[:, 0, :]
+            phase = tables[:, 1, :]
+            bias = tables[:, 2, :]
+
+            amp_max = head.tile([P, Q_TILES], F32)
+            nc.vector.tensor_reduce(
+                out=amp_max[:], in_=amplitude.rearrange("p (s t) -> p t s", t=Q_TILES), axis=AXIS.X, op=ALU.max
+            )
+            shifted = head.tile([P, STATES, Q_TILES], F32)
+            nc.vector.tensor_tensor(
+                out=shifted[:],
+                in0=amplitude.rearrange("p (s t) -> p s t", t=Q_TILES),
+                in1=amp_max[:].unsqueeze(1).to_broadcast([P, STATES, Q_TILES]),
+                op=ALU.subtract,
+            )
+            exps = head.tile([P, STATES, Q_TILES], F32)
+            nc.scalar.activation(out=exps[:], in_=shifted[:], func=ACT.Exp)
+            exp_sum = head.tile([P, Q_TILES], F32)
+            nc.vector.tensor_reduce(out=exp_sum[:], in_=exps[:].rearrange("p s t -> p t s"), axis=AXIS.X, op=ALU.add)
+            inv_sum = head.tile([P, Q_TILES], F32)
+            nc.vector.reciprocal(out=inv_sum[:], in_=exp_sum[:])
+
+            turns = head.tile([P, MIX_COLS], F32)
+            nc.vector.tensor_scalar(out=turns[:], in0=phase, scalar1=1.0 / (2.0 * math.pi), scalar2=None, op0=ALU.mult)
+            whole_int = head.tile([P, MIX_COLS], I32)
+            nc.vector.tensor_copy(out=whole_int[:], in_=turns[:])
+            whole = head.tile([P, MIX_COLS], F32)
+            nc.vector.tensor_copy(out=whole[:], in_=whole_int[:])
+            part_turn = head.tile([P, MIX_COLS], F32)
+            nc.vector.tensor_sub(out=part_turn[:], in0=turns[:], in1=whole[:])
+            half_sin = head.tile([P, MIX_COLS], F32)
+            nc.scalar.activation(out=half_sin[:], in_=part_turn[:], func=ACT.Sin, scale=math.pi)
+            half_sin_sq = head.tile([P, MIX_COLS], F32)
+            nc.vector.tensor_mul(out=half_sin_sq[:], in0=half_sin[:], in1=half_sin[:])
+            cosine = head.tile([P, MIX_COLS], F32)
+            nc.vector.tensor_scalar(
+                out=cosine[:], in0=half_sin_sq[:], scalar1=-2.0, scalar2=1.0, op0=ALU.mult, op1=ALU.add
+            )
+
+            amplitudes = head.tile([P, STATES, Q_TILES], F32)
+            nc.vector.tensor_mul(
+                out=amplitudes[:], in0=exps[:], in1=inv_sum[:].unsqueeze(1).to_broadcast([P, STATES, Q_TILES])
+            )
+            nc.vector.tensor_mul(out=mix[:], in0=amplitudes[:].rearrange("p s t -> p (s t)"), in1=cosine[:])
+            nc.vector.tensor_mul(out=mixed_bias[:], in0=bias, in1=mix[:])
+
+            x_words = x_rows[:].bitcast(F32)
+            grouped = head.tile([P, PASSES, 4 * ROWS], BF16, align_bytes=64)
+            for g in range(PASSES):
+                grouped_words = grouped[:, g, :].bitcast(F32).rearrange("p (r u) -> p r u", u=2)
+                for pair in range(ROW_TILES // 2):
+                    x_cols = head_psum.tile([P, 2, 2 * P], F32, bufs=4)
+                    for u in range(2):
+                        for j in range(2):
+                            nc.tensor.transpose(
+                                out=x_cols[:, u, P * j : P * (j + 1)],
+                                in_=x_words[:, 2 * pair + j, (K_PASS // 2) * g + u : (K_PASS // 2) * (g + 1) : 2],
+                                identity=ident_f32[:],
+                            )
+                    target = grouped_words[:, 2 * P * pair : 2 * P * (pair + 1), :]
+                    if pair % 2 == 0:
+                        nc.vector.tensor_copy(out=target, in_=x_cols[:].rearrange("p u r -> p r u"))
+                    else:
+                        nc.scalar.copy(out=target, in_=x_cols[:].rearrange("p u r -> p r u"))
+            for g in range(PASSES):
+                nc.vector.quantize_mx(
+                    out=x_codes[:, g, :].bitcast(FP8X4), scales=x_scales[:, g, :], in_=grouped[:, g, :]
+                )
+
+        sup_pool = ctx.enter_context(tc.tile_pool(name="sup", bufs=2))
+        work = ctx.enter_context(tc.tile_pool(name="work", bufs=3))
+        small = ctx.enter_context(tc.tile_pool(name="small", bufs=4))
+        acc_psum = ctx.enter_context(tc.psum_pool(name="acc_psum", bufs=4))
+        rows_psum = ctx.enter_context(tc.psum_pool(name="rows_psum", bufs=2))
+
+        def project(s, q_tiles, sup_cols):
+            for t in q_tiles:
+                acc = acc_psum.tile([P, ROWS], F32)
+                for g in range(PASSES):
+                    group = PASSES * s + g
+                    nc.tensor.matmul_mx(
+                        out=acc[:],
+                        lhsT=w_words[:, group, 2 * P * t : 2 * P * (t + 1)].bitcast(FP4X4),
+                        lhsT_scale=w_scales[:, group, P * t : P * (t + 1)],
+                        rhs=x_codes[:, g, :].bitcast(FP8X4),
+                        rhs_scale=x_scales[:, g, :],
+                        start=(g == 0),
+                        stop=(g == PASSES - 1),
+                    )
+                col = Q_TILES * s + t
+                nc.scalar.activation(
+                    out=sup_cols[:, t, :],
+                    in_=acc[:],
+                    func=ACT.Identity,
+                    scale=mix[:, col : col + 1],
+                    bias=mixed_bias[:, col : col + 1],
+                )
+
+        def normalise(s, m, sup_cols):
+            banks = []
+            for h in range(HALVES):
+                sup_rows = rows_psum.tile([P, BANK], F32, name="sup_rows%d" % h)
+                for j in range(TILES_PER_BANK):
+                    nc.tensor.transpose(
+                        out=sup_rows[:, P * j : P * (j + 1)],
+                        in_=sup_cols[:, TILES_PER_BANK * h + j, P * m : P * (m + 1)],
+                        identity=ident_f32[:],
+                    )
+                banks.append(sup_rows)
+
+            stats = small.tile([P, HALVES, BN_STATS_DIM], F32)
+            for h in range(HALVES):
+                nc.vector.bn_stats(out=stats[:, h, :], in_=banks[h][:])
+            mean_var = small.tile([P, 2], F32)
+            nc.vector.bn_aggr(out=mean_var[:], in_=stats[:].rearrange("p h c -> p (h c)"))
+
+            centred = work.tile([P, Q], F32)
+            for h in range(HALVES):
+                cols = slice(BANK * h, BANK * (h + 1))
+                nc.vector.scalar_tensor_tensor(
+                    out=centred[:, cols],
+                    in0=banks[h][:],
+                    scalar=mean_var[:, 0:1],
+                    in1=gamma_all[:, cols],
+                    op0=ALU.subtract,
+                    op1=ALU.mult,
+                )
+
+            inv_std = small.tile([P, 1], F32)
+            nc.scalar.activation(
+                out=inv_std[:], in_=mean_var[:, 1:2], func=ACT.Abs_reciprocal_sqrt, bias=eps[:, 0:1], scale=1.0
+            )
+            scaled = work.tile([P, Q], F32)
+            nc.scalar.activation(out=scaled[:], in_=centred[:], func=ACT.Copy, scale=inv_std[:, 0:1])
+            result = work.tile([P, Q], F32)
+            nc.gpsimd.tensor_tensor(out=result[:], in0=scaled[:], in1=beta_all[:], op=ALU.add)
+            nc.sync.dma_start(out=out[P * m : P * (m + 1), s, :], in_=result[:])
+
+        sup_next = sup_pool.tile([P, Q_TILES, ROWS], F32)
+        project(0, range(Q_TILES), sup_next)
+        for s in range(STATES):
+            sup_now = sup_next
+            if s + 1 < STATES:
+                sup_next = sup_pool.tile([P, Q_TILES, ROWS], F32)
+            for m in range(ROW_TILES):
+                if s + 1 < STATES:
+                    project(s + 1, range(Q_TILES_PER_STEP * m, Q_TILES_PER_STEP * (m + 1)), sup_next)
+                normalise(s, m, sup_now)

@@ -180,79 +180,128 @@ def tile_quantumsuperposition_e_kernel(
         sup_pool = ctx.enter_context(tc.tile_pool(name="sup", bufs=2))
         work = ctx.enter_context(tc.tile_pool(name="work", bufs=3))
         small = ctx.enter_context(tc.tile_pool(name="small", bufs=4))
-        acc_psum = ctx.enter_context(tc.psum_pool(name="acc_psum", bufs=4))
-        rows_psum = ctx.enter_context(tc.psum_pool(name="rows_psum", bufs=2))
+        acc_psum = ctx.enter_context(tc.psum_pool(name="acc_psum", bufs=2))
+        rows_psum = ctx.enter_context(tc.psum_pool(name="rows_psum", bufs=3))
+        ctx.enter_context(tc.manual_schedule())
 
-        def project(s, q_tiles, sup_cols):
-            for t in q_tiles:
-                acc = acc_psum.tile([P, ROWS], F32)
-                for g in range(PASSES):
-                    group = PASSES * s + g
-                    nc.tensor.matmul_mx(
-                        out=acc[:],
-                        lhsT=w_words[:, group, 2 * P * t : 2 * P * (t + 1)].bitcast(FP4X4),
-                        lhsT_scale=w_scales[:, group, P * t : P * (t + 1)],
-                        rhs=x_codes[:, g, :].bitcast(FP8X4),
-                        rhs_scale=x_scales[:, g, :],
-                        start=(g == 0),
-                        stop=(g == PASSES - 1),
-                    )
-                col = Q_TILES * s + t
-                nc.scalar.activation(
-                    out=sup_cols[:, t, :],
-                    in_=acc[:],
-                    func=ACT.Identity,
-                    scale=mix[:, col : col + 1],
-                    bias=mixed_bias[:, col : col + 1],
+        sup = {}
+        rows = {}
+        stats = {}
+        mean_var = {}
+        inv_std = {}
+        centred = {}
+        scaled = {}
+
+        def multiply(s, t):
+            acc = acc_psum.tile([P, ROWS], F32, name="acc")
+            for g in range(PASSES):
+                group = PASSES * s + g
+                nc.tensor.matmul_mx(
+                    out=acc[:],
+                    lhsT=w_words[:, group, 2 * P * t : 2 * P * (t + 1)].bitcast(FP4X4),
+                    lhsT_scale=w_scales[:, group, P * t : P * (t + 1)],
+                    rhs=x_codes[:, g, :].bitcast(FP8X4),
+                    rhs_scale=x_scales[:, g, :],
+                    start=(g == 0),
+                    stop=(g == PASSES - 1),
                 )
+            return acc
 
-        def normalise(s, m, sup_cols):
+        def mix_out(s, t, acc):
+            col = Q_TILES * s + t
+            nc.scalar.activation(
+                out=sup[s][:, t, :],
+                in_=acc[:],
+                func=ACT.Identity,
+                scale=mix[:, col : col + 1],
+                bias=mixed_bias[:, col : col + 1],
+            )
+
+        def new_state(s):
+            sup_cols = sup_pool.tile([P, Q_TILES, ROWS], F32, name="sup_cols")
+            sup[s] = sup_cols
+
+        def turn(i):
+            s, m = divmod(i, ROW_TILES)
             banks = []
             for h in range(HALVES):
                 sup_rows = rows_psum.tile([P, BANK], F32, name="sup_rows%d" % h)
                 for j in range(TILES_PER_BANK):
                     nc.tensor.transpose(
                         out=sup_rows[:, P * j : P * (j + 1)],
-                        in_=sup_cols[:, TILES_PER_BANK * h + j, P * m : P * (m + 1)],
+                        in_=sup[s][:, TILES_PER_BANK * h + j, P * m : P * (m + 1)],
                         identity=ident_f32[:],
                     )
                 banks.append(sup_rows)
+            rows[i] = banks
 
-            stats = small.tile([P, HALVES, BN_STATS_DIM], F32)
+        def measure(i):
+            st = small.tile([P, HALVES, BN_STATS_DIM], F32, name="st")
+            stats[i] = st
             for h in range(HALVES):
-                nc.vector.bn_stats(out=stats[:, h, :], in_=banks[h][:])
-            mean_var = small.tile([P, 2], F32)
-            nc.vector.bn_aggr(out=mean_var[:], in_=stats[:].rearrange("p h c -> p (h c)"))
+                nc.vector.bn_stats(out=st[:, h, :], in_=rows[i][h][:])
 
-            centred = work.tile([P, Q], F32)
+        def aggregate(i):
+            mv = small.tile([P, 2], F32, name="mv")
+            mean_var[i] = mv
+            nc.vector.bn_aggr(out=mv[:], in_=stats[i][:].rearrange("p h c -> p (h c)"))
+
+        def centre(i):
+            cen = work.tile([P, Q], F32, name="cen")
+            centred[i] = cen
             for h in range(HALVES):
                 cols = slice(BANK * h, BANK * (h + 1))
                 nc.vector.scalar_tensor_tensor(
-                    out=centred[:, cols],
-                    in0=banks[h][:],
-                    scalar=mean_var[:, 0:1],
+                    out=cen[:, cols],
+                    in0=rows[i][h][:],
+                    scalar=mean_var[i][:, 0:1],
                     in1=gamma_all[:, cols],
                     op0=ALU.subtract,
                     op1=ALU.mult,
                 )
 
-            inv_std = small.tile([P, 1], F32)
+        def root(i):
+            inv = small.tile([P, 1], F32, name="inv")
+            inv_std[i] = inv
             nc.scalar.activation(
-                out=inv_std[:], in_=mean_var[:, 1:2], func=ACT.Abs_reciprocal_sqrt, bias=eps[:, 0:1], scale=1.0
+                out=inv[:], in_=mean_var[i][:, 1:2], func=ACT.Abs_reciprocal_sqrt, bias=eps[:, 0:1], scale=1.0
             )
-            scaled = work.tile([P, Q], F32)
-            nc.scalar.activation(out=scaled[:], in_=centred[:], func=ACT.Copy, scale=inv_std[:, 0:1])
-            result = work.tile([P, Q], F32)
-            nc.gpsimd.tensor_tensor(out=result[:], in0=scaled[:], in1=beta_all[:], op=ALU.add)
+
+        def scale(i):
+            sca = work.tile([P, Q], F32, name="sca")
+            scaled[i] = sca
+            nc.scalar.activation(out=sca[:], in_=centred[i][:], func=ACT.Copy, scale=inv_std[i][:, 0:1])
+
+        def shift_and_store(i):
+            s, m = divmod(i, ROW_TILES)
+            result = work.tile([P, Q], F32, name="result")
+            nc.gpsimd.tensor_tensor(out=result[:], in0=scaled[i][:], in1=beta_all[:], op=ALU.add)
             nc.sync.dma_start(out=out[P * m : P * (m + 1), s, :], in_=result[:])
 
-        sup_next = sup_pool.tile([P, Q_TILES, ROWS], F32)
-        project(0, range(Q_TILES), sup_next)
-        for s in range(STATES):
-            sup_now = sup_next
-            if s + 1 < STATES:
-                sup_next = sup_pool.tile([P, Q_TILES, ROWS], F32)
-            for m in range(ROW_TILES):
+        UNITS = STATES * ROW_TILES
+        new_state(0)
+        for t in range(Q_TILES):
+            mix_out(0, t, multiply(0, t))
+        for k in range(-2, UNITS + 1):
+            ahead = k + 2
+            products = []
+            if ahead < UNITS:
+                s, m = divmod(ahead, ROW_TILES)
                 if s + 1 < STATES:
-                    project(s + 1, range(Q_TILES_PER_STEP * m, Q_TILES_PER_STEP * (m + 1)), sup_next)
-                normalise(s, m, sup_now)
+                    if m == 0:
+                        new_state(s + 1)
+                    for t in range(Q_TILES_PER_STEP * m, Q_TILES_PER_STEP * (m + 1)):
+                        products.append((s + 1, t, multiply(s + 1, t)))
+                turn(ahead)
+            if 0 <= k + 1 < UNITS:
+                measure(k + 1)
+            if 0 <= k < UNITS:
+                centre(k)
+                root(k)
+            if 0 <= k + 1 < UNITS:
+                aggregate(k + 1)
+            if 0 <= k - 1 < UNITS:
+                scale(k - 1)
+                shift_and_store(k - 1)
+            for s1, t, acc in products:
+                mix_out(s1, t, acc)

@@ -31,6 +31,7 @@ MIX_COLS = STATES * Q_TILES
 Q_TILES_PER_STEP = Q_TILES // ROW_TILES
 BN_STATS_DIM = 6
 LN_EPS = 1e-5
+WARM_UP = 5
 
 FLOPS = 2 * ROWS * STATES * K * Q
 
@@ -50,133 +51,6 @@ def tile_quantumsuperposition_e_kernel(
     nc = tc.nc
     with ExitStack() as ctx:
         keep = ctx.enter_context(tc.tile_pool(name="keep", bufs=1))
-
-        ident_f32 = keep.tile([P, P], F32)
-        make_identity(nc, ident_f32[:])
-        ident_bf16 = keep.tile([P, P], BF16)
-        make_identity(nc, ident_bf16[:])
-        eps = keep.tile([P, 1], F32)
-        nc.vector.memset(eps[:], LN_EPS)
-
-        w_words = keep.tile([P, STATES * PASSES, 2 * Q], U8, align_bytes=64)
-        w_scales = keep.tile([P, STATES * PASSES, Q], U8, align_bytes=64)
-        x_codes = keep.tile([P, PASSES, ROWS], U32, align_bytes=64)
-        x_scales = keep.tile([P, PASSES, ROWS], U8, align_bytes=64)
-
-        mix = keep.tile([P, MIX_COLS], F32)
-        mixed_bias = keep.tile([P, MIX_COLS], F32)
-        gamma_all = keep.tile([P, Q], BF16)
-        beta_all = keep.tile([P, Q], BF16)
-
-        with tc.tile_pool(name="head", bufs=1) as head, tc.psum_pool(name="head_psum", bufs=1) as head_psum:
-            x_rows = head.tile([P, ROW_TILES, K], BF16)
-            for m in range(ROW_TILES):
-                nc.sync.dma_start(out=x_rows[:, m, :], in_=language_features[P * m : P * (m + 1), :])
-
-            for s in range(STATES):
-                groups = slice(PASSES * s, PASSES * (s + 1))
-                nc.sync.dma_start(
-                    out=w_words[:, groups, :].bitcast(I32),
-                    in_=W_words[groups].rearrange("g p c -> p g c").bitcast(I32),
-                )
-                nc.vector.memset(w_scales[:, groups, :].bitcast(I32), 0)
-                for i in range(4):
-                    nc.sync.dma_start(
-                        out=w_scales[32 * i : 32 * i + 4, groups, :].bitcast(I32),
-                        in_=W_scales[groups, 4 * i : 4 * i + 4, :].rearrange("g r n -> r g n").bitcast(I32),
-                    )
-
-            amp_phase_rows = head.tile([P, P], BF16)
-            bias_rows = head.tile([P, P], BF16)
-            nc.vector.memset(bias_rows[MIX_COLS:P, :], 0.0)
-            nc.scalar.dma_start(
-                out=amp_phase_rows[0:MIX_COLS, :], in_=amplitude_weights.rearrange("s (t q) -> (s t) q", q=P)
-            )
-            nc.scalar.dma_start(
-                out=amp_phase_rows[MIX_COLS:P, :], in_=phase_weights.rearrange("s (t q) -> (s t) q", q=P)
-            )
-            nc.scalar.dma_start(out=bias_rows[0:MIX_COLS, :], in_=b.rearrange("s (t q) -> (s t) q", q=P))
-            nc.scalar.dma_start(out=gamma_all[:], in_=ln_gamma.partition_broadcast(P))
-            nc.scalar.dma_start(out=beta_all[:], in_=ln_beta.partition_broadcast(P))
-
-            table_cols = head_psum.tile([P, 4, MIX_COLS], BF16)
-            nc.tensor.transpose(
-                out=table_cols[:, 0:2, :].rearrange("p a c -> p (a c)"), in_=amp_phase_rows[:], identity=ident_bf16[:]
-            )
-            nc.tensor.transpose(
-                out=table_cols[:, 2:4, :].rearrange("p a c -> p (a c)"), in_=bias_rows[:], identity=ident_bf16[:]
-            )
-            tables = head.tile([P, 3, MIX_COLS], F32)
-            nc.vector.tensor_copy(out=tables[:], in_=table_cols[:, 0:3, :])
-            amplitude = tables[:, 0, :]
-            phase = tables[:, 1, :]
-            bias = tables[:, 2, :]
-
-            amp_max = head.tile([P, Q_TILES], F32)
-            nc.vector.tensor_reduce(
-                out=amp_max[:], in_=amplitude.rearrange("p (s t) -> p t s", t=Q_TILES), axis=AXIS.X, op=ALU.max
-            )
-            shifted = head.tile([P, STATES, Q_TILES], F32)
-            nc.vector.tensor_tensor(
-                out=shifted[:],
-                in0=amplitude.rearrange("p (s t) -> p s t", t=Q_TILES),
-                in1=amp_max[:].unsqueeze(1).to_broadcast([P, STATES, Q_TILES]),
-                op=ALU.subtract,
-            )
-            exps = head.tile([P, STATES, Q_TILES], F32)
-            nc.scalar.activation(out=exps[:], in_=shifted[:], func=ACT.Exp)
-            exp_sum = head.tile([P, Q_TILES], F32)
-            nc.vector.tensor_reduce(out=exp_sum[:], in_=exps[:].rearrange("p s t -> p t s"), axis=AXIS.X, op=ALU.add)
-            inv_sum = head.tile([P, Q_TILES], F32)
-            nc.vector.reciprocal(out=inv_sum[:], in_=exp_sum[:])
-
-            turns = head.tile([P, MIX_COLS], F32)
-            nc.vector.tensor_scalar(out=turns[:], in0=phase, scalar1=1.0 / (2.0 * math.pi), scalar2=None, op0=ALU.mult)
-            whole_int = head.tile([P, MIX_COLS], I32)
-            nc.vector.tensor_copy(out=whole_int[:], in_=turns[:])
-            whole = head.tile([P, MIX_COLS], F32)
-            nc.vector.tensor_copy(out=whole[:], in_=whole_int[:])
-            part_turn = head.tile([P, MIX_COLS], F32)
-            nc.vector.tensor_sub(out=part_turn[:], in0=turns[:], in1=whole[:])
-            half_sin = head.tile([P, MIX_COLS], F32)
-            nc.scalar.activation(out=half_sin[:], in_=part_turn[:], func=ACT.Sin, scale=math.pi)
-            half_sin_sq = head.tile([P, MIX_COLS], F32)
-            nc.vector.tensor_mul(out=half_sin_sq[:], in0=half_sin[:], in1=half_sin[:])
-            cosine = head.tile([P, MIX_COLS], F32)
-            nc.vector.tensor_scalar(
-                out=cosine[:], in0=half_sin_sq[:], scalar1=-2.0, scalar2=1.0, op0=ALU.mult, op1=ALU.add
-            )
-
-            amplitudes = head.tile([P, STATES, Q_TILES], F32)
-            nc.vector.tensor_mul(
-                out=amplitudes[:], in0=exps[:], in1=inv_sum[:].unsqueeze(1).to_broadcast([P, STATES, Q_TILES])
-            )
-            nc.vector.tensor_mul(out=mix[:], in0=amplitudes[:].rearrange("p s t -> p (s t)"), in1=cosine[:])
-            nc.vector.tensor_mul(out=mixed_bias[:], in0=bias, in1=mix[:])
-
-            x_words = x_rows[:].bitcast(F32)
-            grouped = head.tile([P, PASSES, 4 * ROWS], BF16, align_bytes=64)
-            for g in range(PASSES):
-                grouped_words = grouped[:, g, :].bitcast(F32).rearrange("p (r u) -> p r u", u=2)
-                for pair in range(ROW_TILES // 2):
-                    x_cols = head_psum.tile([P, 2, 2 * P], F32, bufs=4)
-                    for u in range(2):
-                        for j in range(2):
-                            nc.tensor.transpose(
-                                out=x_cols[:, u, P * j : P * (j + 1)],
-                                in_=x_words[:, 2 * pair + j, (K_PASS // 2) * g + u : (K_PASS // 2) * (g + 1) : 2],
-                                identity=ident_f32[:],
-                            )
-                    target = grouped_words[:, 2 * P * pair : 2 * P * (pair + 1), :]
-                    if pair % 2 == 0:
-                        nc.vector.tensor_copy(out=target, in_=x_cols[:].rearrange("p u r -> p r u"))
-                    else:
-                        nc.scalar.copy(out=target, in_=x_cols[:].rearrange("p u r -> p r u"))
-            for g in range(PASSES):
-                nc.vector.quantize_mx(
-                    out=x_codes[:, g, :].bitcast(FP8X4), scales=x_scales[:, g, :], in_=grouped[:, g, :]
-                )
-
         sup_pool = ctx.enter_context(tc.tile_pool(name="sup", bufs=2))
         work = ctx.enter_context(tc.tile_pool(name="work", bufs=3))
         small = ctx.enter_context(tc.tile_pool(name="small", bufs=4))
@@ -184,16 +58,164 @@ def tile_quantumsuperposition_e_kernel(
         rows_psum = ctx.enter_context(tc.psum_pool(name="rows_psum", bufs=3))
         ctx.enter_context(tc.manual_schedule())
 
+        ident_bf16 = keep.tile([P, P], BF16)
+        make_identity(nc, ident_bf16[:])
+        ident_f32 = keep.tile([P, P], F32)
+        make_identity(nc, ident_f32[:])
+        zeros = keep.tile([P, BANK], BF16)
+        nc.vector.memset(zeros[:], 0.0)
+        eps = keep.tile([P, 1], F32)
+        nc.vector.memset(eps[:], LN_EPS)
+
+        w_words = keep.tile([P, STATES * PASSES, 2 * Q], U8, align_bytes=64)
+        w_scales = keep.tile([P, STATES * PASSES, Q], U8, align_bytes=64)
+        x_codes = keep.tile([P, PASSES, ROWS], U32, align_bytes=64)
+        x_scales = keep.tile([P, PASSES, ROWS], U8, align_bytes=64)
+        mix = keep.tile([P, MIX_COLS], F32)
+        mixed_bias = keep.tile([P, MIX_COLS], F32)
+        gamma_all = keep.tile([P, Q], BF16)
+        beta_all = keep.tile([P, Q], BF16)
+        x_rows = keep.tile([P, ROW_TILES, K], BF16)
+        grouped = keep.tile([P, PASSES, 4 * ROWS], BF16, align_bytes=64)
+        amp_phase_rows = keep.tile([P, P], BF16)
+        bias_rows = keep.tile([P, P], BF16)
+
+        warm = keep.tile([P, 3], F32)
+        nc.scalar.activation(out=warm[:, 0:1], in_=eps[:, 0:1], func=ACT.Exp)
+        idle_bank = acc_psum.tile([P, BANK], F32, name="acc")
+        for i in range(WARM_UP):
+            nc.tensor.matmul(out=idle_bank[:], lhsT=zeros[:, 0:P], rhs=zeros[:], start=True, stop=True)
+
+        nc.vector.memset(w_scales[:, 0:PASSES, :].bitcast(I32), 0)
+        nc.vector.memset(bias_rows[MIX_COLS:P, :], 0.0)
+        nc.gpsimd.memset(w_scales[:, PASSES : STATES * PASSES, :].bitcast(F32), 0.0)
+        nc.sync.dma_start(
+            out=amp_phase_rows[0:MIX_COLS, :], in_=amplitude_weights.rearrange("s (t q) -> (s t) q", q=P)
+        )
+        nc.sync.dma_start(out=amp_phase_rows[MIX_COLS:P, :], in_=phase_weights.rearrange("s (t q) -> (s t) q", q=P))
+        nc.sync.dma_start(out=bias_rows[0:MIX_COLS, :], in_=b.rearrange("s (t q) -> (s t) q", q=P))
+        for m in range(ROW_TILES):
+            nc.sync.dma_start(out=x_rows[:, m, :], in_=language_features[P * m : P * (m + 1), :])
+        for s in range(STATES):
+            groups = slice(PASSES * s, PASSES * (s + 1))
+            for i in range(4):
+                nc.sync.dma_start(
+                    out=w_scales[32 * i : 32 * i + 4, groups, :].bitcast(I32),
+                    in_=W_scales[groups, 4 * i : 4 * i + 4, :].rearrange("g r n -> r g n").bitcast(I32),
+                )
+            nc.sync.dma_start(
+                out=w_words[:, groups, :].bitcast(I32),
+                in_=W_words[groups].rearrange("g p c -> p g c").bitcast(I32),
+            )
+            if s == 1:
+                nc.sync.dma_start(out=gamma_all[:], in_=ln_gamma.partition_broadcast(P))
+                nc.sync.dma_start(out=beta_all[:], in_=ln_beta.partition_broadcast(P))
+
+        table_cols = acc_psum.tile([P, 4, MIX_COLS], BF16, name="acc")
+        nc.tensor.transpose(
+            out=table_cols[:, 0:2, :].rearrange("p a c -> p (a c)"), in_=amp_phase_rows[:], identity=ident_bf16[:]
+        )
+        nc.tensor.transpose(
+            out=table_cols[:, 2:4, :].rearrange("p a c -> p (a c)"), in_=bias_rows[:], identity=ident_bf16[:]
+        )
+        tables = keep.tile([P, 3, MIX_COLS], F32)
+        nc.vector.tensor_copy(out=tables[:], in_=table_cols[:, 0:3, :])
+        amplitude = tables[:, 0, :]
+        phase = tables[:, 1, :]
+        bias = tables[:, 2, :]
+        amp_max = keep.tile([P, Q_TILES], F32)
+        nc.vector.tensor_reduce(
+            out=amp_max[:], in_=amplitude.rearrange("p (s t) -> p t s", t=Q_TILES), axis=AXIS.X, op=ALU.max
+        )
+        shifted = keep.tile([P, STATES, Q_TILES], F32)
+        nc.vector.tensor_tensor(
+            out=shifted[:],
+            in0=amplitude.rearrange("p (s t) -> p s t", t=Q_TILES),
+            in1=amp_max[:].unsqueeze(1).to_broadcast([P, STATES, Q_TILES]),
+            op=ALU.subtract,
+        )
+        whole_int = keep.tile([P, MIX_COLS], I32)
+        nc.vector.tensor_scalar(
+            out=whole_int[:], in0=phase, scalar1=1.0 / (2.0 * math.pi), scalar2=None, op0=ALU.mult
+        )
+        part_turn = keep.tile([P, MIX_COLS], F32)
+        nc.vector.scalar_tensor_tensor(
+            out=part_turn[:],
+            in0=phase,
+            scalar=1.0 / (2.0 * math.pi),
+            in1=whole_int[:],
+            op0=ALU.mult,
+            op1=ALU.subtract,
+        )
+
+        x_words = x_rows[:].bitcast(F32)
+        grouped_words = grouped[:].bitcast(F32).rearrange("p g (r u) -> p g r u", u=2)
+
+        def turn_x(m):
+            x_cols = rows_psum.tile([P, PASSES, 2, P], F32, name="sup_rows%d" % (m % HALVES))
+            for g in range(PASSES):
+                for u in range(2):
+                    nc.tensor.transpose(
+                        out=x_cols[:, g, u, :],
+                        in_=x_words[:, m, (K_PASS // 2) * g + u : (K_PASS // 2) * (g + 1) : 2],
+                        identity=ident_f32[:],
+                    )
+            return x_cols
+
+        def quantise_x(first, count):
+            for g in range(PASSES):
+                nc.vector.quantize_mx(
+                    out=x_codes[:, g, P * first : P * (first + count)].bitcast(FP8X4),
+                    scales=x_scales[:, g, P * first : P * (first + count)],
+                    in_=grouped[:, g, 4 * P * first : 4 * P * (first + count)],
+                )
+
+        for m in range(ROW_TILES):
+            x_cols = turn_x(m)
+            target = grouped_words[:, :, P * m : P * (m + 1), :]
+            nc.scalar.copy(out=target, in_=x_cols[:].rearrange("p g u r -> p g r u"))
+        exps = keep.tile([P, STATES, Q_TILES], F32)
+        nc.scalar.activation(out=exps[:], in_=shifted[:], func=ACT.Exp)
+        half_sin = keep.tile([P, MIX_COLS], F32)
+        nc.scalar.activation(out=half_sin[:], in_=part_turn[:], func=ACT.Sin, scale=math.pi)
+        nc.scalar.activation(out=warm[:, 1:2], in_=eps[:, 0:1], func=ACT.Abs_reciprocal_sqrt)
+
+        quantise_x(0, 2)
+        quantise_x(2, 2)
+
+        exp_sum = keep.tile([P, Q_TILES], F32)
+        nc.vector.tensor_reduce(out=exp_sum[:], in_=exps[:].rearrange("p s t -> p t s"), axis=AXIS.X, op=ALU.add)
+        inv_sum = keep.tile([P, Q_TILES], F32)
+        nc.vector.reciprocal(out=inv_sum[:], in_=exp_sum[:])
+        amplitudes = keep.tile([P, STATES, Q_TILES], F32)
+        nc.vector.tensor_mul(
+            out=amplitudes[:], in0=exps[:], in1=inv_sum[:].unsqueeze(1).to_broadcast([P, STATES, Q_TILES])
+        )
+        minus_two_sin_sq = keep.tile([P, MIX_COLS], F32)
+        nc.vector.scalar_tensor_tensor(
+            out=minus_two_sin_sq[:], in0=half_sin[:], scalar=-2.0, in1=half_sin[:], op0=ALU.mult, op1=ALU.mult
+        )
+        nc.vector.scalar_tensor_tensor(
+            out=mix[:],
+            in0=minus_two_sin_sq[:],
+            scalar=1.0,
+            in1=amplitudes[:].rearrange("p s t -> p (s t)"),
+            op0=ALU.add,
+            op1=ALU.mult,
+        )
+        nc.vector.tensor_mul(out=mixed_bias[:], in0=bias, in1=mix[:])
+
         sup = {}
         rows = {}
         stats = {}
         mean_var = {}
         inv_std = {}
         centred = {}
-        scaled = {}
+        UNITS = STATES * ROW_TILES
+        ON_VECTOR = 2
 
-        def multiply(s, t):
-            acc = acc_psum.tile([P, ROWS], F32, name="acc")
+        def multiply(s, t, pool, tag):
+            acc = pool.tile([P, ROWS], F32, name=tag)
             for g in range(PASSES):
                 group = PASSES * s + g
                 nc.tensor.matmul_mx(
@@ -205,21 +227,41 @@ def tile_quantumsuperposition_e_kernel(
                     start=(g == 0),
                     stop=(g == PASSES - 1),
                 )
-            return acc
+            return (s, t, acc)
 
-        def mix_out(s, t, acc):
+        def mix_out(product, on_vector=False):
+            s, t, acc = product
             col = Q_TILES * s + t
-            nc.scalar.activation(
-                out=sup[s][:, t, :],
-                in_=acc[:],
-                func=ACT.Identity,
-                scale=mix[:, col : col + 1],
-                bias=mixed_bias[:, col : col + 1],
-            )
+            if on_vector:
+                nc.vector.tensor_scalar(
+                    out=sup[s][:, t, :],
+                    in0=acc[:],
+                    scalar1=mix[:, col : col + 1],
+                    scalar2=mixed_bias[:, col : col + 1],
+                    op0=ALU.mult,
+                    op1=ALU.add,
+                )
+            else:
+                nc.scalar.activation(
+                    out=sup[s][:, t, :],
+                    in_=acc[:],
+                    func=ACT.Identity,
+                    scale=mix[:, col : col + 1],
+                    bias=mixed_bias[:, col : col + 1],
+                )
 
         def new_state(s):
             sup_cols = sup_pool.tile([P, Q_TILES, ROWS], F32, name="sup_cols")
             sup[s] = sup_cols
+
+        def pair(s, m):
+            if m == 0:
+                new_state(s)
+            return [multiply(s, Q_TILES_PER_STEP * m + j, acc_psum, "acc") for j in range(Q_TILES_PER_STEP)]
+
+        def pair_out(products):
+            for product in products:
+                mix_out(product)
 
         def turn(i):
             s, m = divmod(i, ROW_TILES)
@@ -267,41 +309,93 @@ def tile_quantumsuperposition_e_kernel(
                 out=inv[:], in_=mean_var[i][:, 1:2], func=ACT.Abs_reciprocal_sqrt, bias=eps[:, 0:1], scale=1.0
             )
 
-        def scale(i):
-            sca = work.tile([P, Q], F32, name="sca")
-            scaled[i] = sca
-            nc.scalar.activation(out=sca[:], in_=centred[i][:], func=ACT.Copy, scale=inv_std[i][:, 0:1])
-
-        def shift_and_store(i):
+        def finish(i):
             s, m = divmod(i, ROW_TILES)
+            sca = work.tile([P, Q], F32, name="sca")
+            nc.scalar.activation(out=sca[:], in_=centred[i][:], func=ACT.Copy, scale=inv_std[i][:, 0:1])
             result = work.tile([P, Q], F32, name="result")
-            nc.gpsimd.tensor_tensor(out=result[:], in0=scaled[i][:], in1=beta_all[:], op=ALU.add)
+            nc.gpsimd.tensor_tensor(out=result[:], in0=sca[:], in1=beta_all[:], op=ALU.add)
             nc.sync.dma_start(out=out[P * m : P * (m + 1), s, :], in_=result[:])
 
-        UNITS = STATES * ROW_TILES
+        def finish_on_vector(i, beta_banks):
+            s, m = divmod(i, ROW_TILES)
+            result = work.tile([P, Q], F32, name="result")
+            for h in range(HALVES):
+                cols = slice(BANK * h, BANK * (h + 1))
+                nc.vector.scalar_tensor_tensor(
+                    out=result[:, cols],
+                    in0=centred[i][:, cols],
+                    scalar=inv_std[i][:, 0:1],
+                    in1=beta_banks[h][:],
+                    op0=ALU.mult,
+                    op1=ALU.add,
+                )
+                queue = nc.sync if h == 0 else nc.scalar
+                queue.dma_start(out=out[P * m : P * (m + 1), s, cols], in_=result[:, cols])
+
         new_state(0)
         for t in range(Q_TILES):
-            mix_out(0, t, multiply(0, t))
-        for k in range(-2, UNITS + 1):
+            if t < 2:
+                product = multiply(0, t, acc_psum, "acc")
+            else:
+                product = multiply(0, t, rows_psum, "sup_rows%d" % (t % 2))
+            mix_out(product, on_vector=(t % 2 == 0))
+
+        turn(0)
+        products = pair(1, 0)
+        measure(0)
+        aggregate(0)
+        pair_out(products)
+        turn(1)
+        turn(2)
+        centre(0)
+        root(0)
+        finish(0)
+        products = pair(1, 1)
+        pair_out(products)
+        measure(1)
+        aggregate(1)
+        root(1)
+        products = pair(1, 2)
+        pair_out(products)
+        turn(3)
+        measure(2)
+        centre(1)
+        aggregate(2)
+        finish(1)
+        products = pair(1, 3)
+        pair_out(products)
+
+        beta_banks = []
+        for k in range(2, UNITS):
             ahead = k + 2
             products = []
             if ahead < UNITS:
                 s, m = divmod(ahead, ROW_TILES)
                 if s + 1 < STATES:
-                    if m == 0:
-                        new_state(s + 1)
-                    for t in range(Q_TILES_PER_STEP * m, Q_TILES_PER_STEP * (m + 1)):
-                        products.append((s + 1, t, multiply(s + 1, t)))
+                    products = pair(s + 1, m)
+                elif m == 0:
+                    for h in range(HALVES):
+                        beta_bank = acc_psum.tile([P, BANK], F32, name="acc")
+                        nc.tensor.matmul(
+                            out=beta_bank[:],
+                            lhsT=ident_bf16[:],
+                            rhs=beta_all[:, BANK * h : BANK * (h + 1)],
+                            start=True,
+                            stop=True,
+                        )
+                        beta_banks.append(beta_bank)
                 turn(ahead)
-            if 0 <= k + 1 < UNITS:
+            if k + 1 < UNITS:
                 measure(k + 1)
-            if 0 <= k < UNITS:
-                centre(k)
-                root(k)
-            if 0 <= k + 1 < UNITS:
+            centre(k)
+            root(k)
+            if k + 1 < UNITS:
                 aggregate(k + 1)
-            if 0 <= k - 1 < UNITS:
-                scale(k - 1)
-                shift_and_store(k - 1)
-            for s1, t, acc in products:
-                mix_out(s1, t, acc)
+            if k > 2:
+                if k - 1 < UNITS - ON_VECTOR:
+                    finish(k - 1)
+                else:
+                    finish_on_vector(k - 1, beta_banks)
+            pair_out(products)
+        finish_on_vector(UNITS - 1, beta_banks)

@@ -212,7 +212,7 @@ def tile_quantumsuperposition_e_kernel(
         inv_std = {}
         centred = {}
         UNITS = STATES * ROW_TILES
-        ON_VECTOR = 2
+        ON_VECTOR = 3
 
         def multiply(s, t, pool, tag):
             acc = pool.tile([P, ROWS], F32, name=tag)

@@ -32,6 +32,7 @@ Q_TILES_PER_STEP = Q_TILES // ROW_TILES
 BN_STATS_DIM = 6
 LN_EPS = 1e-5
 WARM_UP = 5
+KEEP_WARM = 4
 
 FLOPS = 2 * ROWS * STATES * K * Q
 
@@ -178,7 +179,9 @@ def tile_quantumsuperposition_e_kernel(
         nc.scalar.activation(out=exps[:], in_=shifted[:], func=ACT.Exp)
         half_sin = keep.tile([P, MIX_COLS], F32)
         nc.scalar.activation(out=half_sin[:], in_=part_turn[:], func=ACT.Sin, scale=math.pi)
-        nc.scalar.activation(out=warm[:, 1:2], in_=eps[:, 0:1], func=ACT.Abs_reciprocal_sqrt)
+        idle_bank = acc_psum.tile([P, BANK], F32, name="acc")
+        for i in range(KEEP_WARM):
+            nc.tensor.matmul(out=idle_bank[:], lhsT=zeros[:, 0:P], rhs=zeros[:], start=True, stop=True)
 
         quantise_x(0, 2)
         quantise_x(2, 2)
@@ -211,7 +214,9 @@ def tile_quantumsuperposition_e_kernel(
         mean_var = {}
         inv_std = {}
         centred = {}
+        neg_mean = {}
         UNITS = STATES * ROW_TILES
+        ON_SCALAR = (UNITS - 3, UNITS - 1)
         ON_VECTOR = 3
 
         def multiply(s, t, pool, tag):
@@ -296,9 +301,9 @@ def tile_quantumsuperposition_e_kernel(
                 nc.vector.scalar_tensor_tensor(
                     out=cen[:, cols],
                     in0=rows[i][h][:],
-                    scalar=mean_var[i][:, 0:1],
+                    scalar=(neg_mean[i][:, 0:1] if i in ON_SCALAR else mean_var[i][:, 0:1]),
                     in1=gamma_all[:, cols],
-                    op0=ALU.subtract,
+                    op0=(ALU.add if i in ON_SCALAR else ALU.subtract),
                     op1=ALU.mult,
                 )
 
@@ -307,6 +312,41 @@ def tile_quantumsuperposition_e_kernel(
             inv_std[i] = inv
             nc.scalar.activation(
                 out=inv[:], in_=mean_var[i][:, 1:2], func=ACT.Abs_reciprocal_sqrt, bias=eps[:, 0:1], scale=1.0
+            )
+
+        def measure_on_scalar(i):
+            sums = small.tile([P, 2 * HALVES], F32, name="sums")
+            folded = small.tile([P, 2 * HALVES], F32, name="folded")
+            for h in range(HALVES):
+                unused = work.tile([P, BANK], F32, name="unused")
+                nc.scalar.activation(out=unused[:], in_=rows[i][h][:], func=ACT.Copy, accum_out=sums[:, h : h + 1])
+            neg = small.tile([P, 1], F32, name="neg")
+            neg_mean[i] = neg
+            nc.scalar.activation(
+                out=folded[:, 0:HALVES], in_=sums[:, 0:HALVES], func=ACT.Copy, scale=-1.0 / Q, accum_out=neg[:]
+            )
+            for h in range(HALVES):
+                unused = work.tile([P, BANK], F32, name="unused")
+                nc.scalar.activation(
+                    out=unused[:],
+                    in_=rows[i][h][:],
+                    func=ACT.Square,
+                    bias=neg[:, 0:1],
+                    scale=1.0,
+                    accum_out=sums[:, HALVES + h : HALVES + h + 1],
+                )
+            var = small.tile([P, 1], F32, name="var")
+            nc.scalar.activation(
+                out=folded[:, HALVES : 2 * HALVES],
+                in_=sums[:, HALVES : 2 * HALVES],
+                func=ACT.Copy,
+                scale=1.0 / Q,
+                accum_out=var[:],
+            )
+            inv = small.tile([P, 1], F32, name="inv")
+            inv_std[i] = inv
+            nc.scalar.activation(
+                out=inv[:], in_=var[:, 0:1], func=ACT.Abs_reciprocal_sqrt, bias=eps[:, 0:1], scale=1.0
             )
 
         def finish(i):
@@ -319,7 +359,7 @@ def tile_quantumsuperposition_e_kernel(
 
         def finish_on_vector(i, beta_banks):
             s, m = divmod(i, ROW_TILES)
-            result = work.tile([P, Q], F32, name="result")
+            result = work.tile([P, Q], F32, name="late_result")
             for h in range(HALVES):
                 cols = slice(BANK * h, BANK * (h + 1))
                 nc.vector.scalar_tensor_tensor(
@@ -340,6 +380,7 @@ def tile_quantumsuperposition_e_kernel(
             else:
                 product = multiply(0, t, rows_psum, "sup_rows%d" % (t % 2))
             mix_out(product, on_vector=(t % 2 == 0))
+        nc.scalar.activation(out=warm[:, 1:2], in_=eps[:, 0:1], func=ACT.Abs_reciprocal_sqrt)
 
         turn(0)
         products = pair(1, 0)
@@ -386,11 +427,13 @@ def tile_quantumsuperposition_e_kernel(
                         )
                         beta_banks.append(beta_bank)
                 turn(ahead)
-            if k + 1 < UNITS:
+            on_vector = k + 1 < UNITS and k + 1 not in ON_SCALAR
+            if on_vector:
                 measure(k + 1)
             centre(k)
-            root(k)
-            if k + 1 < UNITS:
+            if k not in ON_SCALAR:
+                root(k)
+            if on_vector:
                 aggregate(k + 1)
             if k > 2:
                 if k - 1 < UNITS - ON_VECTOR:
@@ -398,4 +441,6 @@ def tile_quantumsuperposition_e_kernel(
                 else:
                     finish_on_vector(k - 1, beta_banks)
             pair_out(products)
+            if ahead in ON_SCALAR:
+                measure_on_scalar(ahead)
         finish_on_vector(UNITS - 1, beta_banks)

@@ -217,7 +217,7 @@ def tile_quantumsuperposition_e_kernel(
         neg_mean = {}
         UNITS = STATES * ROW_TILES
         ON_SCALAR = (UNITS - 3, UNITS - 1)
-        ON_VECTOR = 3
+        ON_VECTOR = 4
 
         def multiply(s, t, pool, tag):
             acc = pool.tile([P, ROWS], F32, name=tag)

import math
from contextlib import ExitStack

import concourse.mybir as mybir
from concourse.masks import make_identity

F32 = mybir.dt.float32
BF16 = mybir.dt.bfloat16
I32 = mybir.dt.int32
U32 = mybir.dt.uint32
U8 = mybir.dt.uint8
FP8X4 = mybir.dt.float8_e4m3fn_x4
FP4X4 = mybir.dt.float4_e2m1fn_x4
ALU = mybir.AluOpType
ACT = mybir.ActivationFunctionType
AXIS = mybir.AxisListType

P = 128
ROWS = 512
STATES = 8
K = 1024
Q = 1024
K_PASS = 4 * P
PASSES = K // K_PASS
ROW_TILES = ROWS // P
Q_TILES = Q // P
BANK = 512
HALVES = Q // BANK
TILES_PER_BANK = BANK // P
MIX_COLS = STATES * Q_TILES
Q_TILES_PER_STEP = Q_TILES // ROW_TILES
BN_STATS_DIM = 6
LN_EPS = 1e-5
WARM_UP = 5
KEEP_WARM = 4

FLOPS = 2 * ROWS * STATES * K * Q


def tile_quantumsuperposition_e_kernel(
    tc,
    language_features,
    W_words,
    W_scales,
    b,
    amplitude_weights,
    phase_weights,
    ln_gamma,
    ln_beta,
    out,
):
    nc = tc.nc
    with ExitStack() as ctx:
        keep = ctx.enter_context(tc.tile_pool(name="keep", bufs=1))
        sup_pool = ctx.enter_context(tc.tile_pool(name="sup", bufs=2))
        work = ctx.enter_context(tc.tile_pool(name="work", bufs=3))
        small = ctx.enter_context(tc.tile_pool(name="small", bufs=4))
        acc_psum = ctx.enter_context(tc.psum_pool(name="acc_psum", bufs=2))
        rows_psum = ctx.enter_context(tc.psum_pool(name="rows_psum", bufs=3))
        ctx.enter_context(tc.manual_schedule())

        ident_bf16 = keep.tile([P, P], BF16)
        make_identity(nc, ident_bf16[:])
        ident_f32 = keep.tile([P, P], F32)
        make_identity(nc, ident_f32[:])
        zeros = keep.tile([P, BANK], BF16)
        nc.vector.memset(zeros[:], 0.0)
        eps = keep.tile([P, 1], F32)
        nc.vector.memset(eps[:], LN_EPS)

        w_words = keep.tile([P, STATES * PASSES, 2 * Q], U8, align_bytes=64)
        w_scales = keep.tile([P, STATES * PASSES, Q], U8, align_bytes=64)
        x_codes = keep.tile([P, PASSES, ROWS], U32, align_bytes=64)
        x_scales = keep.tile([P, PASSES, ROWS], U8, align_bytes=64)
        mix = keep.tile([P, MIX_COLS], F32)
        mixed_bias = keep.tile([P, MIX_COLS], F32)
        gamma_all = keep.tile([P, Q], BF16)
        beta_all = keep.tile([P, Q], BF16)
        x_rows = keep.tile([P, ROW_TILES, K], BF16)
        grouped = keep.tile([P, PASSES, 4 * ROWS], BF16, align_bytes=64)
        amp_phase_rows = keep.tile([P, P], BF16)
        bias_rows = keep.tile([P, P], BF16)

        warm = keep.tile([P, 3], F32)
        nc.scalar.activation(out=warm[:, 0:1], in_=eps[:, 0:1], func=ACT.Exp)
        idle_bank = acc_psum.tile([P, BANK], F32, name="acc")
        for i in range(WARM_UP):
            nc.tensor.matmul(out=idle_bank[:], lhsT=zeros[:, 0:P], rhs=zeros[:], start=True, stop=True)

        nc.vector.memset(w_scales[:, 0:PASSES, :].bitcast(I32), 0)
        nc.vector.memset(bias_rows[MIX_COLS:P, :], 0.0)
        nc.gpsimd.memset(w_scales[:, PASSES : STATES * PASSES, :].bitcast(F32), 0.0)
        nc.sync.dma_start(
            out=amp_phase_rows[0:MIX_COLS, :], in_=amplitude_weights.rearrange("s (t q) -> (s t) q", q=P)
        )
        nc.sync.dma_start(out=amp_phase_rows[MIX_COLS:P, :], in_=phase_weights.rearrange("s (t q) -> (s t) q", q=P))
        nc.sync.dma_start(out=bias_rows[0:MIX_COLS, :], in_=b.rearrange("s (t q) -> (s t) q", q=P))
        for m in range(ROW_TILES):
            nc.sync.dma_start(out=x_rows[:, m, :], in_=language_features[P * m : P * (m + 1), :])
        for s in range(STATES):
            groups = slice(PASSES * s, PASSES * (s + 1))
            for i in range(4):
                nc.sync.dma_start(
                    out=w_scales[32 * i : 32 * i + 4, groups, :].bitcast(I32),
                    in_=W_scales[groups, 4 * i : 4 * i + 4, :].rearrange("g r n -> r g n").bitcast(I32),
                )
            nc.sync.dma_start(
                out=w_words[:, groups, :].bitcast(I32),
                in_=W_words[groups].rearrange("g p c -> p g c").bitcast(I32),
            )
            if s == 1:
                nc.sync.dma_start(out=gamma_all[:], in_=ln_gamma.partition_broadcast(P))
                nc.sync.dma_start(out=beta_all[:], in_=ln_beta.partition_broadcast(P))

        table_cols = acc_psum.tile([P, 4, MIX_COLS], BF16, name="acc")
        nc.tensor.transpose(
            out=table_cols[:, 0:2, :].rearrange("p a c -> p (a c)"), in_=amp_phase_rows[:], identity=ident_bf16[:]
        )
        nc.tensor.transpose(
            out=table_cols[:, 2:4, :].rearrange("p a c -> p (a c)"), in_=bias_rows[:], identity=ident_bf16[:]
        )
        tables = keep.tile([P, 3, MIX_COLS], F32)
        nc.vector.tensor_copy(out=tables[:], in_=table_cols[:, 0:3, :])
        amplitude = tables[:, 0, :]
        phase = tables[:, 1, :]
        bias = tables[:, 2, :]
        amp_max = keep.tile([P, Q_TILES], F32)
        nc.vector.tensor_reduce(
            out=amp_max[:], in_=amplitude.rearrange("p (s t) -> p t s", t=Q_TILES), axis=AXIS.X, op=ALU.max
        )
        shifted = keep.tile([P, STATES, Q_TILES], F32)
        nc.vector.tensor_tensor(
            out=shifted[:],
            in0=amplitude.rearrange("p (s t) -> p s t", t=Q_TILES),
            in1=amp_max[:].unsqueeze(1).to_broadcast([P, STATES, Q_TILES]),
            op=ALU.subtract,
        )
        whole_int = keep.tile([P, MIX_COLS], I32)
        nc.vector.tensor_scalar(
            out=whole_int[:], in0=phase, scalar1=1.0 / (2.0 * math.pi), scalar2=None, op0=ALU.mult
        )
        part_turn = keep.tile([P, MIX_COLS], F32)
        nc.vector.scalar_tensor_tensor(
            out=part_turn[:],
            in0=phase,
            scalar=1.0 / (2.0 * math.pi),
            in1=whole_int[:],
            op0=ALU.mult,
            op1=ALU.subtract,
        )

        x_words = x_rows[:].bitcast(F32)
        grouped_words = grouped[:].bitcast(F32).rearrange("p g (r u) -> p g r u", u=2)

        def turn_x(m):
            x_cols = rows_psum.tile([P, PASSES, 2, P], F32, name="sup_rows%d" % (m % HALVES))
            for g in range(PASSES):
                for u in range(2):
                    nc.tensor.transpose(
                        out=x_cols[:, g, u, :],
                        in_=x_words[:, m, (K_PASS // 2) * g + u : (K_PASS // 2) * (g + 1) : 2],
                        identity=ident_f32[:],
                    )
            return x_cols

        def quantise_x(first, count):
            for g in range(PASSES):
                nc.vector.quantize_mx(
                    out=x_codes[:, g, P * first : P * (first + count)].bitcast(FP8X4),
                    scales=x_scales[:, g, P * first : P * (first + count)],
                    in_=grouped[:, g, 4 * P * first : 4 * P * (first + count)],
                )

        for m in range(ROW_TILES):
            x_cols = turn_x(m)
            target = grouped_words[:, :, P * m : P * (m + 1), :]
            nc.scalar.copy(out=target, in_=x_cols[:].rearrange("p g u r -> p g r u"))
        exps = keep.tile([P, STATES, Q_TILES], F32)
        nc.scalar.activation(out=exps[:], in_=shifted[:], func=ACT.Exp)
        half_sin = keep.tile([P, MIX_COLS], F32)
        nc.scalar.activation(out=half_sin[:], in_=part_turn[:], func=ACT.Sin, scale=math.pi)
        idle_bank = acc_psum.tile([P, BANK], F32, name="acc")
        for i in range(KEEP_WARM):
            nc.tensor.matmul(out=idle_bank[:], lhsT=zeros[:, 0:P], rhs=zeros[:], start=True, stop=True)

        quantise_x(0, 2)
        quantise_x(2, 2)

        exp_sum = keep.tile([P, Q_TILES], F32)
        nc.vector.tensor_reduce(out=exp_sum[:], in_=exps[:].rearrange("p s t -> p t s"), axis=AXIS.X, op=ALU.add)
        inv_sum = keep.tile([P, Q_TILES], F32)
        nc.vector.reciprocal(out=inv_sum[:], in_=exp_sum[:])
        amplitudes = keep.tile([P, STATES, Q_TILES], F32)
        nc.vector.tensor_mul(
            out=amplitudes[:], in0=exps[:], in1=inv_sum[:].unsqueeze(1).to_broadcast([P, STATES, Q_TILES])
        )
        minus_two_sin_sq = keep.tile([P, MIX_COLS], F32)
        nc.vector.scalar_tensor_tensor(
            out=minus_two_sin_sq[:], in0=half_sin[:], scalar=-2.0, in1=half_sin[:], op0=ALU.mult, op1=ALU.mult
        )
        nc.vector.scalar_tensor_tensor(
            out=mix[:],
            in0=minus_two_sin_sq[:],
            scalar=1.0,
            in1=amplitudes[:].rearrange("p s t -> p (s t)"),
            op0=ALU.add,
            op1=ALU.mult,
        )
        nc.vector.tensor_mul(out=mixed_bias[:], in0=bias, in1=mix[:])

        sup = {}
        rows = {}
        stats = {}
        mean_var = {}
        inv_std = {}
        centred = {}
        neg_mean = {}
        UNITS = STATES * ROW_TILES
        ON_SCALAR = (UNITS - 3, UNITS - 1)
        ON_VECTOR = 4

        def multiply(s, t, pool, tag):
            acc = pool.tile([P, ROWS], F32, name=tag)
            for g in range(PASSES):
                group = PASSES * s + g
                nc.tensor.matmul_mx(
                    out=acc[:],
                    lhsT=w_words[:, group, 2 * P * t : 2 * P * (t + 1)].bitcast(FP4X4),
                    lhsT_scale=w_scales[:, group, P * t : P * (t + 1)],
                    rhs=x_codes[:, g, :].bitcast(FP8X4),
                    rhs_scale=x_scales[:, g, :],
                    start=(g == 0),
                    stop=(g == PASSES - 1),
                )
            return (s, t, acc)

        def mix_out(product, on_vector=False):
            s, t, acc = product
            col = Q_TILES * s + t
            if on_vector:
                nc.vector.tensor_scalar(
                    out=sup[s][:, t, :],
                    in0=acc[:],
                    scalar1=mix[:, col : col + 1],
                    scalar2=mixed_bias[:, col : col + 1],
                    op0=ALU.mult,
                    op1=ALU.add,
                )
            else:
                nc.scalar.activation(
                    out=sup[s][:, t, :],
                    in_=acc[:],
                    func=ACT.Identity,
                    scale=mix[:, col : col + 1],
                    bias=mixed_bias[:, col : col + 1],
                )

        def new_state(s):
            sup_cols = sup_pool.tile([P, Q_TILES, ROWS], F32, name="sup_cols")
            sup[s] = sup_cols

        def pair(s, m):
            if m == 0:
                new_state(s)
            return [multiply(s, Q_TILES_PER_STEP * m + j, acc_psum, "acc") for j in range(Q_TILES_PER_STEP)]

        def pair_out(products):
            for product in products:
                mix_out(product)

        def turn(i):
            s, m = divmod(i, ROW_TILES)
            banks = []
            for h in range(HALVES):
                sup_rows = rows_psum.tile([P, BANK], F32, name="sup_rows%d" % h)
                for j in range(TILES_PER_BANK):
                    nc.tensor.transpose(
                        out=sup_rows[:, P * j : P * (j + 1)],
                        in_=sup[s][:, TILES_PER_BANK * h + j, P * m : P * (m + 1)],
                        identity=ident_f32[:],
                    )
                banks.append(sup_rows)
            rows[i] = banks

        def measure(i):
            st = small.tile([P, HALVES, BN_STATS_DIM], F32, name="st")
            stats[i] = st
            for h in range(HALVES):
                nc.vector.bn_stats(out=st[:, h, :], in_=rows[i][h][:])

        def aggregate(i):
            mv = small.tile([P, 2], F32, name="mv")
            mean_var[i] = mv
            nc.vector.bn_aggr(out=mv[:], in_=stats[i][:].rearrange("p h c -> p (h c)"))

        def centre(i):
            cen = work.tile([P, Q], F32, name="cen")
            centred[i] = cen
            for h in range(HALVES):
                cols = slice(BANK * h, BANK * (h + 1))
                nc.vector.scalar_tensor_tensor(
                    out=cen[:, cols],
                    in0=rows[i][h][:],
                    scalar=(neg_mean[i][:, 0:1] if i in ON_SCALAR else mean_var[i][:, 0:1]),
                    in1=gamma_all[:, cols],
                    op0=(ALU.add if i in ON_SCALAR else ALU.subtract),
                    op1=ALU.mult,
                )

        def root(i):
            inv = small.tile([P, 1], F32, name="inv")
            inv_std[i] = inv
            nc.scalar.activation(
                out=inv[:], in_=mean_var[i][:, 1:2], func=ACT.Abs_reciprocal_sqrt, bias=eps[:, 0:1], scale=1.0
            )

        def measure_on_scalar(i):
            sums = small.tile([P, 2 * HALVES], F32, name="sums")
            folded = small.tile([P, 2 * HALVES], F32, name="folded")
            for h in range(HALVES):
                unused = work.tile([P, BANK], F32, name="unused")
                nc.scalar.activation(out=unused[:], in_=rows[i][h][:], func=ACT.Copy, accum_out=sums[:, h : h + 1])
            neg = small.tile([P, 1], F32, name="neg")
            neg_mean[i] = neg
            nc.scalar.activation(
                out=folded[:, 0:HALVES], in_=sums[:, 0:HALVES], func=ACT.Copy, scale=-1.0 / Q, accum_out=neg[:]
            )
            for h in range(HALVES):
                unused = work.tile([P, BANK], F32, name="unused")
                nc.scalar.activation(
                    out=unused[:],
                    in_=rows[i][h][:],
                    func=ACT.Square,
                    bias=neg[:, 0:1],
                    scale=1.0,
                    accum_out=sums[:, HALVES + h : HALVES + h + 1],
                )
            var = small.tile([P, 1], F32, name="var")
            nc.scalar.activation(
                out=folded[:, HALVES : 2 * HALVES],
                in_=sums[:, HALVES : 2 * HALVES],
                func=ACT.Copy,
                scale=1.0 / Q,
                accum_out=var[:],
            )
            inv = small.tile([P, 1], F32, name="inv")
            inv_std[i] = inv
            nc.scalar.activation(
                out=inv[:], in_=var[:, 0:1], func=ACT.Abs_reciprocal_sqrt, bias=eps[:, 0:1], scale=1.0
            )

        def finish(i):
            s, m = divmod(i, ROW_TILES)
            sca = work.tile([P, Q], F32, name="sca")
            nc.scalar.activation(out=sca[:], in_=centred[i][:], func=ACT.Copy, scale=inv_std[i][:, 0:1])
            result = work.tile([P, Q], F32, name="result")
            nc.gpsimd.tensor_tensor(out=result[:], in0=sca[:], in1=beta_all[:], op=ALU.add)
            nc.sync.dma_start(out=out[P * m : P * (m + 1), s, :], in_=result[:])

        def finish_on_vector(i, beta_banks):
            s, m = divmod(i, ROW_TILES)
            result = work.tile([P, Q], F32, name="late_result")
            for h in range(HALVES):
                cols = slice(BANK * h, BANK * (h + 1))
                nc.vector.scalar_tensor_tensor(
                    out=result[:, cols],
                    in0=centred[i][:, cols],
                    scalar=inv_std[i][:, 0:1],
                    in1=beta_banks[h][:],
                    op0=ALU.mult,
                    op1=ALU.add,
                )
                queue = nc.sync if h == 0 else nc.scalar
                queue.dma_start(out=out[P * m : P * (m + 1), s, cols], in_=result[:, cols])

        new_state(0)
        for t in range(Q_TILES):
            if t < 2:
                product = multiply(0, t, acc_psum, "acc")
            else:
                product = multiply(0, t, rows_psum, "sup_rows%d" % (t % 2))
            mix_out(product, on_vector=(t % 2 == 0))
        nc.scalar.activation(out=warm[:, 1:2], in_=eps[:, 0:1], func=ACT.Abs_reciprocal_sqrt)

        turn(0)
        products = pair(1, 0)
        measure(0)
        aggregate(0)
        pair_out(products)
        turn(1)
        turn(2)
        centre(0)
        root(0)
        finish(0)
        products = pair(1, 1)
        pair_out(products)
        measure(1)
        aggregate(1)
        root(1)
        products = pair(1, 2)
        pair_out(products)
        turn(3)
        measure(2)
        centre(1)
        aggregate(2)
        finish(1)
        products = pair(1, 3)
        pair_out(products)

        beta_banks = []
        for k in range(2, UNITS):
            ahead = k + 2
            products = []
            if ahead < UNITS:
                s, m = divmod(ahead, ROW_TILES)
                if s + 1 < STATES:
                    products = pair(s + 1, m)
                elif m == 0:
                    for h in range(HALVES):
                        beta_bank = acc_psum.tile([P, BANK], F32, name="acc")
                        nc.tensor.matmul(
                            out=beta_bank[:],
                            lhsT=ident_bf16[:],
                            rhs=beta_all[:, BANK * h : BANK * (h + 1)],
                            start=True,
                            stop=True,
                        )
                        beta_banks.append(beta_bank)
                turn(ahead)
            on_vector = k + 1 < UNITS and k + 1 not in ON_SCALAR
            if on_vector:
                measure(k + 1)
            centre(k)
            if k not in ON_SCALAR:
                root(k)
            if on_vector:
                aggregate(k + 1)
            if k > 2:
                if k - 1 < UNITS - ON_VECTOR:
                    finish(k - 1)
                else:
                    finish_on_vector(k - 1, beta_banks)
            pair_out(products)
            if ahead in ON_SCALAR:
                measure_on_scalar(ahead)
        finish_on_vector(UNITS - 1, beta_banks)
